import numpy as np
import ml_dtypes


def mxq(x, axis, fmt="e4m3"):
    dtype, down = {"e4m3": (ml_dtypes.float8_e4m3fn, 7), "e5m2": (ml_dtypes.float8_e5m2, 14)}[fmt]
    v = np.moveaxis(np.asarray(x, np.float32).astype(ml_dtypes.bfloat16).astype(np.float64), axis, -1)
    blocks = v.reshape(v.shape[:-1] + (-1, 32))
    amax = np.abs(blocks).max(-1, keepdims=True)
    byte = np.maximum(np.where(amax > 0, np.frexp(amax)[1] - 1 + 127, 0) - down, 1)
    scale = np.exp2(byte - 127.0)
    codes = (blocks / scale).astype(np.float32).astype(dtype).astype(np.float64)
    return np.moveaxis((codes * scale).reshape(v.shape), -1, axis)


WIDE = False


def mx_kscale(k):
    if not WIDE:
        return np.ones(k)
    levels = np.array([10, -10, 5, -5, 0])
    a = np.random.permutation(np.resize(levels, k // 512 * 4)).reshape(k // 512, 4)
    idx = np.arange(k)
    return np.exp2(a[idx // 512, idx % 128 // 32])


BF16 = ml_dtypes.bfloat16


def bf(x):
    return np.asarray(x, np.float32).astype(BF16)


def f64(x):
    return np.asarray(x).astype(np.float64)


B, C, H, W = 4, 512, 32, 32
N = H * W
C3 = 3 * C
EPS = 1e-4


def weight_norm(v, g):
    return g[:, None] * v / np.sqrt((v * v).sum(axis=1, keepdims=True))


def setup_inputs():
    s = mx_kscale(C)
    lift = np.sqrt(np.mean(1.0 / (s * s)))
    amp = np.exp2(-2.0 - 7.0 * np.random.random((B, 1, H, W)))
    row = np.exp(0.5 * np.random.standard_normal((C3, 1)))
    return {"x": bf(np.random.standard_normal((B, C, H, W)) * amp * (s * lift)[None, :, None, None]),
            "v_qkv": bf(np.random.standard_normal((C3, C)) * row / np.sqrt(C) / s[None, :]),
            "g_qkv": bf(1.0 + 0.1 * np.random.standard_normal(C3))}


def reference(x, v_qkv, g_qkv):
    w = weight_norm(f64(v_qkv), f64(g_qkv))
    xt = f64(x).reshape(B, C, N)
    qkv = mxq(w, 1, "e4m3") @ mxq(xt, 1, "e4m3")
    rms = np.sqrt(np.mean(np.square(qkv), axis=1, keepdims=True)) + EPS
    return qkv / rms

@@ -1,0 +1,242 @@
+from contextlib import ExitStack
+import math
+
+import concourse.mybir as mybir
+from concourse.masks import make_identity
+
+F32 = mybir.dt.float32
+BF16 = mybir.dt.bfloat16
+U32 = mybir.dt.uint32
+U8 = mybir.dt.uint8
+FP8X4 = mybir.dt.float8_e4m3fn_x4
+ACT = mybir.ActivationFunctionType
+ALU = mybir.AluOpType
+AX = mybir.AxisListType
+
+B, C, N, O = 4, 512, 1024, 1536
+P = 128
+PACK = 4
+J = O // P
+HALF = 512
+EPS = 1e-4
+FLOPS = 2 * B * O * C * N
+
+LEAD = 6
+V_TILES = (1, 3, 5)
+G_FROM = 27
+PIN = False
+
+
+def tile_admattentionblock_pa_t_kernel(tc, x, v_qkv, g_qkv, out):
+    nc = tc.nc
+    with ExitStack() as ctx:
+        if PIN:
+            ctx.enter_context(tc.manual_schedule())
+        keep = ctx.enter_context(tc.tile_pool(name="keep", bufs=1))
+        work = ctx.enter_context(tc.tile_pool(name="work", bufs=2))
+        stage = ctx.enter_context(tc.tile_pool(name="stage", bufs=6))
+        psum = ctx.enter_context(tc.psum_pool(name="psum", bufs=1))
+
+        g_sb = keep.tile([P, J], BF16)
+        nc.sync.dma_start(out=g_sb[:], in_=g_qkv.rearrange("(p j) -> p j", j=J))
+        v_sb = keep.tile([P, J, C], BF16)
+        v_view = v_qkv.rearrange("(p j) c -> p j c", j=J)
+        for a in range(3):
+            nc.sync.dma_start(out=v_sb[:, 4 * a:4 * a + 4, :], in_=v_view[:, 4 * a:4 * a + 4, :])
+        x_raw = []
+        for b in range(B):
+            xr = keep.tile([P, PACK, N], BF16, name="x_raw%d" % b)
+            nc.sync.dma_start(out=xr[:], in_=x[b].rearrange("(p t) h w -> p t (h w)", t=PACK))
+            x_raw.append(xr)
+
+        ident_bf = keep.tile([P, P], BF16)
+        make_identity(nc, ident_bf[:])
+        ident_f = keep.tile([P, P], F32)
+        make_identity(nc, ident_f[:])
+        one = keep.tile([P, 1], F32)
+        nc.vector.memset(one[:], 1.0)
+        warm = keep.tile([P, 1], F32)
+        nc.scalar.activation(out=warm[:], in_=one[:], func=ACT.Sqrt)
+
+        xc = [keep.tile([P, N], U32, align_bytes=64, name="xc%d" % b) for b in range(B)]
+        xs = [keep.tile([P, N], U8, align_bytes=64, name="xs%d" % b) for b in range(B)]
+        xgs = {}
+
+        def regroup_x(b, h):
+            xg = work.tile([P, HALF, PACK], BF16, align_bytes=64, tag="xg", bufs=4, name="xg")
+            src = x_raw[b][:, :, HALF * h:HALF * (h + 1)]
+            if b == 0:
+                nc.vector.tensor_copy(out=xg[:].rearrange("p (c i) t -> p c t i", i=4),
+                                      in_=src.rearrange("p t (c i) -> p c t i", i=4))
+            else:
+                nc.gpsimd.tensor_scalar(out=xg[:], in0=src.rearrange("p t n -> p n t"),
+                                        scalar1=1.0, scalar2=0.0, op0=ALU.mult, op1=ALU.add)
+            xgs[(b, h)] = xg
+
+        def quantise_x(b, h):
+            nc.vector.quantize_mx(
+                out=xc[b][:, HALF * h:HALF * (h + 1)].bitcast(FP8X4),
+                scales=xs[b][:, HALF * h:HALF * (h + 1)],
+                in_=xgs[(b, h)][:].rearrange("p n t -> p (n t)"))
+
+        ss = keep.tile([P, 3, 16], F32)
+        norm = keep.tile([P, J], F32)
+        rnorm = keep.tile([P, J], F32)
+        sc = keep.tile([P, J], F32)
+        w_bf = keep.tile([P, J, PACK, P], BF16)
+        wg = keep.tile([P, J, P, PACK], BF16, align_bytes=64)
+        wc = keep.tile([P, O], U32, align_bytes=64)
+        ws = keep.tile([P, O], U8, align_bytes=64)
+        for a in range(3):
+            for r in range(4):
+                j = 4 * a + r
+                if r < 2:
+                    junk_s = work.tile([P, C], BF16, tag="junk_s")
+                    nc.scalar.activation(out=junk_s[:], in_=v_sb[:, j, :], func=ACT.Square,
+                                         accum_out=ss[:, a, r:r + 1])
+                else:
+                    junk_v = work.tile([P, C], F32, tag="junk_v")
+                    nc.vector.scalar_tensor_tensor(out=junk_v[:], in0=v_sb[:, j, :], scalar=1.0,
+                                                   in1=v_sb[:, j, :], op0=ALU.mult, op1=ALU.mult,
+                                                   accum_out=ss[:, a, 6 + r:7 + r])
+            four = slice(4 * a, 4 * a + 4)
+            nc.scalar.activation(out=norm[:, four].rearrange("p (s e) -> p s e", e=2),
+                                 in_=ss[:, a, :].rearrange("p (s e) -> p s e", e=8)[:, :, 0:2],
+                                 func=ACT.Sqrt)
+            nc.vector.reciprocal(out=rnorm[:, four], in_=norm[:, four])
+            nc.vector.tensor_tensor(out=sc[:, four], in0=rnorm[:, four], in1=g_sb[:, four], op=ALU.mult)
+            for r in range(4):
+                j = 4 * a + r
+                v_perm = v_sb[:, j, :].rearrange("p (c t) -> p t c", t=PACK)
+                if r < 3:
+                    nc.vector.tensor_scalar(out=w_bf[:, j], in0=v_perm, scalar1=sc[:, j:j + 1],
+                                            scalar2=None, op0=ALU.mult)
+                else:
+                    nc.scalar.activation(out=w_bf[:, j], in_=v_perm, func=ACT.Copy,
+                                         scale=sc[:, j:j + 1])
+                wt = psum.tile([P, PACK, P], BF16, tag="mm", bufs=4)
+                for t in range(PACK):
+                    nc.tensor.transpose(out=wt[:, t, :], in_=w_bf[:, j, t, :], identity=ident_bf[:])
+                if r == 1:
+                    nc.vector.tensor_copy(out=wg[:, j], in_=wt[:].rearrange("p t o -> p o t"))
+                else:
+                    nc.scalar.copy(out=wg[:, j], in_=wt[:].rearrange("p t o -> p o t"))
+            if a == 1:
+                regroup_x(0, 0)
+            nc.vector.quantize_mx(
+                out=wc[:, HALF * a:HALF * (a + 1)].bitcast(FP8X4),
+                scales=ws[:, HALF * a:HALF * (a + 1)],
+                in_=wg[:, 4 * a:4 * a + 4].rearrange("p j o t -> p (j o t)"))
+        quantise_x(0, 0)
+        regroup_x(0, 1)
+        for b in range(1, B):
+            for h in range(2):
+                regroup_x(b, h)
+
+        inv_sqrt_o = 1.0 / math.sqrt(O)
+        rb = {}
+        state = {}
+
+        def mx(ps, lw, lcols, rw, rcols):
+            nc.tensor.matmul_mx(out=ps[:], lhsT=lw[0][:, lcols].bitcast(FP8X4), lhsT_scale=lw[1][:, lcols],
+                                rhs=rw[0][:, rcols].bitcast(FP8X4), rhs_scale=rw[1][:, rcols],
+                                start=True, stop=True)
+
+        def square_bank(k, g):
+            b, i = divmod(k, 8)
+            ii = i % 4
+            if ii == 0 and g == 0:
+                state["acc"] = work.tile([P, 12], F32, tag="acc", name="acc")
+                state["ms"] = work.tile([P, 4], F32, tag="ms", name="ms")
+            ps = psum.tile([P, HALF], F32, tag="sq", bufs=3, name="ps_sq")
+            mx(ps, (xc[b], xs[b]), slice(P * i, P * (i + 1)), (wc, ws), slice(HALF * g, HALF * (g + 1)))
+            if k in V_TILES:
+                if g == 0:
+                    state["st"] = work.tile([P, 3, 6], F32, tag="st", name="st")
+                nc.vector.bn_stats(out=state["st"][:, g, :], in_=ps[:])
+                if g == 2:
+                    mv = work.tile([P, 2], F32, tag="mv")
+                    nc.vector.bn_aggr(out=mv[:], in_=state["st"][:].rearrange("p g s -> p (g s)"))
+                    nc.vector.scalar_tensor_tensor(out=state["ms"][:, ii:ii + 1], in0=mv[:, 0:1],
+                                                   scalar=mv[:, 0:1], in1=mv[:, 1:2],
+                                                   op0=ALU.mult, op1=ALU.add)
+            else:
+                junk = work.tile([P, HALF], BF16, tag="junk")
+                nc.scalar.activation(out=junk[:], in_=ps[:], func=ACT.Square, scale=inv_sqrt_o,
+                                     accum_out=state["acc"][:, 3 * ii + g:3 * ii + g + 1])
+                if g == 2:
+                    nc.vector.tensor_reduce(out=state["ms"][:, ii:ii + 1],
+                                            in_=state["acc"][:, 3 * ii:3 * ii + 3],
+                                            axis=AX.X, op=ALU.add)
+
+        def chain_a():
+            rms = work.tile([P, 4], F32, tag="rms")
+            nc.scalar.activation(out=rms[:], in_=state["ms"][:], func=ACT.Sqrt)
+            rme = work.tile([P, 4], F32, tag="rme")
+            nc.vector.tensor_scalar_add(out=rme[:], in0=rms[:], scalar1=EPS)
+            rinv = work.tile([P, 4], F32, tag="rinv", name="rinv")
+            nc.vector.reciprocal(out=rinv[:], in_=rme[:])
+            state["rinv"] = rinv
+
+        def chain_b(u):
+            bc = psum.tile([P, HALF], F32, tag="bc", bufs=1)
+            for q in range(4):
+                nc.tensor.transpose(out=bc[:, P * q:P * (q + 1)],
+                                    in_=state["rinv"][:, q:q + 1].to_broadcast([P, P]),
+                                    identity=ident_f[:])
+            r = work.tile([P, HALF], F32, tag="rb", bufs=4, name="rb")
+            nc.scalar.copy(out=r[:], in_=bc[:])
+            rb[u] = r
+
+        items = [(0, q, h) for h in range(2) for q in range(4)]
+        for b in range(1, B - 1):
+            items += [(b, 0, 0), (b, 1, 0), (b, 2, 0), (b, 0, 1), (b, 1, 1), (b, 2, 1), (b, 3, 0), (b, 3, 1)]
+        items += [(B - 1, q, h) for h in range(2) for q in range(4)]
+        ots = {}
+
+        def final_bank(m, jj):
+            b, q, h = items[m]
+            j = 3 * q + jj
+            o_view = out[b].rearrange("(p j) n -> p j n", j=J)
+            split = b == 0 or b == B - 1
+            if split:
+                if jj == 0:
+                    ots[(b, q)] = stage.tile([P, 3, HALF], F32, tag="ot", name="ot0")
+                dst = ots[(b, q)][:, jj, :]
+            else:
+                if jj == 0 and h == 0:
+                    ots[(b, q)] = stage.tile([P, 3, N], F32, tag="ot", name="ot")
+                dst = ots[(b, q)][:, jj, HALF * h:HALF * (h + 1)]
+            ps = psum.tile([P, HALF], F32, tag="mm", bufs=4, name="ps_mm")
+            mx(ps, (wc, ws), slice(P * j, P * (j + 1)), (xc[b], xs[b]), slice(HALF * h, HALF * (h + 1)))
+            if m >= G_FROM and jj == 0:
+                nc.scalar.copy(out=dst, in_=ps[:])
+                nc.gpsimd.tensor_tensor(out=dst, in0=dst, in1=rb[2 * b + h][:], op=ALU.mult)
+            else:
+                nc.vector.tensor_tensor(out=dst, in0=ps[:], in1=rb[2 * b + h][:], op=ALU.mult)
+            if m == len(items) - 1:
+                nc.sync.dma_start(out=o_view[:, j:j + 1, HALF * h:HALF * (h + 1)],
+                                  in_=ots[(b, q)][:, jj:jj + 1, :])
+            elif split:
+                if jj == 2:
+                    nc.sync.dma_start(out=o_view[:, 3 * q:3 * q + 3, HALF * h:HALF * (h + 1)],
+                                      in_=ots[(b, q)][:])
+            elif h == 1 and jj == 2:
+                nc.sync.dma_start(out=o_view[:, 3 * q:3 * q + 3, :], in_=ots[(b, q)][:])
+
+        n_tiles = 8 * B
+        for r in range(n_tiles + LEAD):
+            for g in range(3):
+                if r < n_tiles:
+                    square_bank(r, g)
+                if r >= LEAD:
+                    final_bank(r - LEAD, g)
+            if r == 0:
+                quantise_x(0, 1)
+            if r < n_tiles and r % 4 == 3:
+                chain_a()
+            if 0 < r <= n_tiles and r % 4 == 0:
+                chain_b(r // 4 - 1)
+            if r % 4 == 1 and r // 4 + 2 < 2 * B:
+                u = r // 4 + 2
+                quantise_x(u // 2, u % 2)

@@ -22,8 +22,8 @@ EPS = 1e-4
 FLOPS = 2 * B * O * C * N
 
 LEAD = 6
-V_TILES = (1, 3, 5)
-G_FROM = 27
+V_TILES = (1, 3)
+G_FROM = 19
 PIN = False
 
 
@@ -38,7 +38,7 @@ def tile_admattentionblock_pa_t_kernel(tc, x, v_qkv, g_qkv, out):
         psum = ctx.enter_context(tc.psum_pool(name="psum", bufs=1))
 
         g_sb = keep.tile([P, J], BF16)
-        nc.sync.dma_start(out=g_sb[:], in_=g_qkv.rearrange("(p j) -> p j", j=J))
+        nc.scalar.dma_start(out=g_sb[:], in_=g_qkv.rearrange("(p j) -> p j", j=J))
         v_sb = keep.tile([P, J, C], BF16)
         v_view = v_qkv.rearrange("(p j) c -> p j c", j=J)
         for a in range(3):
@@ -65,7 +65,7 @@ def tile_admattentionblock_pa_t_kernel(tc, x, v_qkv, g_qkv, out):
         def regroup_x(b, h):
             xg = work.tile([P, HALF, PACK], BF16, align_bytes=64, tag="xg", bufs=4, name="xg")
             src = x_raw[b][:, :, HALF * h:HALF * (h + 1)]
-            if b == 0:
+            if b >= 0:
                 nc.vector.tensor_copy(out=xg[:].rearrange("p (c i) t -> p c t i", i=4),
                                       in_=src.rearrange("p t (c i) -> p c t i", i=4))
             else:
@@ -129,9 +129,6 @@ def tile_admattentionblock_pa_t_kernel(tc, x, v_qkv, g_qkv, out):
                 in_=wg[:, 4 * a:4 * a + 4].rearrange("p j o t -> p (j o t)"))
         quantise_x(0, 0)
         regroup_x(0, 1)
-        for b in range(1, B):
-            for h in range(2):
-                regroup_x(b, h)
 
         inv_sqrt_o = 1.0 / math.sqrt(O)
         rb = {}
@@ -189,16 +186,15 @@ def tile_admattentionblock_pa_t_kernel(tc, x, v_qkv, g_qkv, out):
             rb[u] = r
 
         items = [(0, q, h) for h in range(2) for q in range(4)]
-        for b in range(1, B - 1):
-            items += [(b, 0, 0), (b, 1, 0), (b, 2, 0), (b, 0, 1), (b, 1, 1), (b, 2, 1), (b, 3, 0), (b, 3, 1)]
-        items += [(B - 1, q, h) for h in range(2) for q in range(4)]
+        for b in range(1, B):
+            items += [(b, q, h) for h in range(2) for q in range(4)]
         ots = {}
 
         def final_bank(m, jj):
             b, q, h = items[m]
             j = 3 * q + jj
             o_view = out[b].rearrange("(p j) n -> p j n", j=J)
-            split = b == 0 or b == B - 1
+            split = True
             if split:
                 if jj == 0:
                     ots[(b, q)] = stage.tile([P, 3, HALF], F32, tag="ot", name="ot0")
@@ -233,6 +229,7 @@ def tile_admattentionblock_pa_t_kernel(tc, x, v_qkv, g_qkv, out):
                     final_bank(r - LEAD, g)
             if r == 0:
                 quantise_x(0, 1)
+                regroup_x(1, 0)
             if r < n_tiles and r % 4 == 3:
                 chain_a()
             if 0 < r <= n_tiles and r % 4 == 0:
@@ -240,3 +237,5 @@ def tile_admattentionblock_pa_t_kernel(tc, x, v_qkv, g_qkv, out):
             if r % 4 == 1 and r // 4 + 2 < 2 * B:
                 u = r // 4 + 2
                 quantise_x(u // 2, u % 2)
+                if u + 1 < 2 * B:
+                    regroup_x((u + 1) // 2, (u + 1) % 2)

@@ -22,8 +22,8 @@ EPS = 1e-4
 FLOPS = 2 * B * O * C * N
 
 LEAD = 6
-V_TILES = (1, 3)
-G_FROM = 19
+V_TILES = (1, 3, 9, 13, 21)
+G_LAST = 13
 PIN = False
 
 
@@ -34,7 +34,7 @@ def tile_admattentionblock_pa_t_kernel(tc, x, v_qkv, g_qkv, out):
             ctx.enter_context(tc.manual_schedule())
         keep = ctx.enter_context(tc.tile_pool(name="keep", bufs=1))
         work = ctx.enter_context(tc.tile_pool(name="work", bufs=2))
-        stage = ctx.enter_context(tc.tile_pool(name="stage", bufs=6))
+        stage = ctx.enter_context(tc.tile_pool(name="stage", bufs=8))
         psum = ctx.enter_context(tc.psum_pool(name="psum", bufs=1))
 
         g_sb = keep.tile([P, J], BF16)
@@ -63,9 +63,9 @@ def tile_admattentionblock_pa_t_kernel(tc, x, v_qkv, g_qkv, out):
         xgs = {}
 
         def regroup_x(b, h):
-            xg = work.tile([P, HALF, PACK], BF16, align_bytes=64, tag="xg", bufs=4, name="xg")
+            xg = work.tile([P, HALF, PACK], BF16, align_bytes=64, tag="xg", bufs=1, name="xg")
             src = x_raw[b][:, :, HALF * h:HALF * (h + 1)]
-            if b >= 0:
+            if b == 0:
                 nc.vector.tensor_copy(out=xg[:].rearrange("p (c i) t -> p c t i", i=4),
                                       in_=src.rearrange("p t (c i) -> p c t i", i=4))
             else:
@@ -128,11 +128,20 @@ def tile_admattentionblock_pa_t_kernel(tc, x, v_qkv, g_qkv, out):
                 scales=ws[:, HALF * a:HALF * (a + 1)],
                 in_=wg[:, 4 * a:4 * a + 4].rearrange("p j o t -> p (j o t)"))
         quantise_x(0, 0)
-        regroup_x(0, 1)
 
         inv_sqrt_o = 1.0 / math.sqrt(O)
+        units = [(0, 0, 2), (0, 2 * P, 2), (0, HALF, 4)]
+        units += [(b, HALF * h, 4) for b in range(1, B) for h in range(2)]
+        unit_of_tile = []
+        for u in range(len(units)):
+            unit_of_tile += [u] * units[u][2]
+        first_tile = [unit_of_tile.index(u) for u in range(len(units))]
+        n_tiles = len(unit_of_tile)
         rb = {}
-        state = {}
+        accs = {}
+        mss = {}
+        sts = {}
+        rinvs = {}
 
         def mx(ps, lw, lcols, rw, rcols):
             nc.tensor.matmul_mx(out=ps[:], lhsT=lw[0][:, lcols].bitcast(FP8X4), lhsT_scale=lw[1][:, lcols],
@@ -141,101 +150,123 @@ def tile_admattentionblock_pa_t_kernel(tc, x, v_qkv, g_qkv, out):
 
         def square_bank(k, g):
             b, i = divmod(k, 8)
-            ii = i % 4
-            if ii == 0 and g == 0:
-                state["acc"] = work.tile([P, 12], F32, tag="acc", name="acc")
-                state["ms"] = work.tile([P, 4], F32, tag="ms", name="ms")
-            ps = psum.tile([P, HALF], F32, tag="sq", bufs=3, name="ps_sq")
+            u = unit_of_tile[k]
+            ii = k - first_tile[u]
+            nt = units[u][2]
+            if u not in accs:
+                accs[u] = work.tile([P, 3 * nt], F32, tag="acc", name="acc")
+                mss[u] = work.tile([P, nt], F32, tag="ms", name="ms")
+            on_vector = k in V_TILES
+            if on_vector:
+                ps = psum.tile([P, HALF], F32, tag="mm", bufs=4, name="ps_sv")
+            else:
+                ps = psum.tile([P, HALF], F32, tag="sq", bufs=3, name="ps_sq")
             mx(ps, (xc[b], xs[b]), slice(P * i, P * (i + 1)), (wc, ws), slice(HALF * g, HALF * (g + 1)))
-            if k in V_TILES:
+            if on_vector:
                 if g == 0:
-                    state["st"] = work.tile([P, 3, 6], F32, tag="st", name="st")
-                nc.vector.bn_stats(out=state["st"][:, g, :], in_=ps[:])
+                    sts[k] = work.tile([P, 3, 6], F32, tag="st", name="st")
+                nc.vector.bn_stats(out=sts[k][:, g, :], in_=ps[:])
                 if g == 2:
                     mv = work.tile([P, 2], F32, tag="mv")
-                    nc.vector.bn_aggr(out=mv[:], in_=state["st"][:].rearrange("p g s -> p (g s)"))
-                    nc.vector.scalar_tensor_tensor(out=state["ms"][:, ii:ii + 1], in0=mv[:, 0:1],
+                    nc.vector.bn_aggr(out=mv[:], in_=sts[k][:].rearrange("p g s -> p (g s)"))
+                    nc.vector.scalar_tensor_tensor(out=mss[u][:, ii:ii + 1], in0=mv[:, 0:1],
                                                    scalar=mv[:, 0:1], in1=mv[:, 1:2],
                                                    op0=ALU.mult, op1=ALU.add)
             else:
                 junk = work.tile([P, HALF], BF16, tag="junk")
                 nc.scalar.activation(out=junk[:], in_=ps[:], func=ACT.Square, scale=inv_sqrt_o,
-                                     accum_out=state["acc"][:, 3 * ii + g:3 * ii + g + 1])
-                if g == 2:
-                    nc.vector.tensor_reduce(out=state["ms"][:, ii:ii + 1],
-                                            in_=state["acc"][:, 3 * ii:3 * ii + 3],
-                                            axis=AX.X, op=ALU.add)
+                                     accum_out=accs[u][:, 3 * ii + g:3 * ii + g + 1])
+                first = ii
+                while first > 0 and (k - (ii - first) - 1) not in V_TILES:
+                    first -= 1
+                if g == 2 and (ii == nt - 1 or (k + 1) in V_TILES):
+                    nc.vector.tensor_reduce(
+                        out=mss[u][:, first:ii + 1],
+                        in_=accs[u][:, 3 * first:3 * ii + 3].rearrange("p (i g) -> p i g", g=3),
+                        axis=AX.X, op=ALU.add)
 
-        def chain_a():
-            rms = work.tile([P, 4], F32, tag="rms")
-            nc.scalar.activation(out=rms[:], in_=state["ms"][:], func=ACT.Sqrt)
-            rme = work.tile([P, 4], F32, tag="rme")
+        def chain_a(u):
+            nt = units[u][2]
+            rms = work.tile([P, nt], F32, tag="rms")
+            nc.scalar.activation(out=rms[:], in_=mss[u][:], func=ACT.Sqrt)
+            rme = work.tile([P, nt], F32, tag="rme")
             nc.vector.tensor_scalar_add(out=rme[:], in0=rms[:], scalar1=EPS)
-            rinv = work.tile([P, 4], F32, tag="rinv", name="rinv")
-            nc.vector.reciprocal(out=rinv[:], in_=rme[:])
-            state["rinv"] = rinv
+            rinvs[u] = work.tile([P, nt], F32, tag="rinv", name="rinv")
+            nc.vector.reciprocal(out=rinvs[u][:], in_=rme[:])
 
         def chain_b(u):
-            bc = psum.tile([P, HALF], F32, tag="bc", bufs=1)
-            for q in range(4):
+            nt = units[u][2]
+            bc = psum.tile([P, P * nt], F32, tag="bc", bufs=1)
+            for q in range(nt):
                 nc.tensor.transpose(out=bc[:, P * q:P * (q + 1)],
-                                    in_=state["rinv"][:, q:q + 1].to_broadcast([P, P]),
+                                    in_=rinvs[u][:, q:q + 1].to_broadcast([P, P]),
                                     identity=ident_f[:])
-            r = work.tile([P, HALF], F32, tag="rb", bufs=4, name="rb")
-            nc.scalar.copy(out=r[:], in_=bc[:])
-            rb[u] = r
+            rb[u] = work.tile([P, P * nt], F32, tag="rb", bufs=4, name="rb")
+            if u < 2:
+                nc.vector.tensor_copy(out=rb[u][:], in_=bc[:])
+            else:
+                nc.scalar.copy(out=rb[u][:], in_=bc[:])
 
-        items = [(0, q, h) for h in range(2) for q in range(4)]
-        for b in range(1, B):
-            items += [(b, q, h) for h in range(2) for q in range(4)]
+        items = [(u, q) for u in range(len(units)) for q in range(4)]
         ots = {}
 
         def final_bank(m, jj):
-            b, q, h = items[m]
+            u, q = items[m]
+            b, n0, nt = units[u]
+            width = P * nt
             j = 3 * q + jj
+            cols = slice(n0, n0 + width)
             o_view = out[b].rearrange("(p j) n -> p j n", j=J)
-            split = True
-            if split:
-                if jj == 0:
-                    ots[(b, q)] = stage.tile([P, 3, HALF], F32, tag="ot", name="ot0")
-                dst = ots[(b, q)][:, jj, :]
-            else:
-                if jj == 0 and h == 0:
-                    ots[(b, q)] = stage.tile([P, 3, N], F32, tag="ot", name="ot")
-                dst = ots[(b, q)][:, jj, HALF * h:HALF * (h + 1)]
-            ps = psum.tile([P, HALF], F32, tag="mm", bufs=4, name="ps_mm")
-            mx(ps, (wc, ws), slice(P * j, P * (j + 1)), (xc[b], xs[b]), slice(HALF * h, HALF * (h + 1)))
-            if m >= G_FROM and jj == 0:
+            if jj == 0:
+                ots[m] = stage.tile([P, 3, width], F32, tag="ot", name="ot")
+            dst = ots[m][:, jj, :]
+            ps = psum.tile([P, width], F32, tag="mm", bufs=4, name="ps_mm")
+            mx(ps, (wc, ws), slice(P * j, P * (j + 1)), (xc[b], xs[b]), cols)
+            if m >= len(items) - G_LAST and jj == 0:
                 nc.scalar.copy(out=dst, in_=ps[:])
-                nc.gpsimd.tensor_tensor(out=dst, in0=dst, in1=rb[2 * b + h][:], op=ALU.mult)
+                nc.gpsimd.tensor_tensor(out=dst, in0=dst, in1=rb[u][:], op=ALU.mult)
             else:
-                nc.vector.tensor_tensor(out=dst, in0=ps[:], in1=rb[2 * b + h][:], op=ALU.mult)
+                nc.vector.tensor_tensor(out=dst, in0=ps[:], in1=rb[u][:], op=ALU.mult)
             if m == len(items) - 1:
-                nc.sync.dma_start(out=o_view[:, j:j + 1, HALF * h:HALF * (h + 1)],
-                                  in_=ots[(b, q)][:, jj:jj + 1, :])
-            elif split:
-                if jj == 2:
-                    nc.sync.dma_start(out=o_view[:, 3 * q:3 * q + 3, HALF * h:HALF * (h + 1)],
-                                      in_=ots[(b, q)][:])
-            elif h == 1 and jj == 2:
-                nc.sync.dma_start(out=o_view[:, 3 * q:3 * q + 3, :], in_=ots[(b, q)][:])
+                nc.sync.dma_start(out=o_view[:, j:j + 1, cols], in_=ots[m][:, jj:jj + 1, :])
+            elif jj == 2:
+                nc.sync.dma_start(out=o_view[:, 3 * q:3 * q + 3, cols], in_=ots[m][:])
 
-        n_tiles = 8 * B
-        for r in range(n_tiles + LEAD):
+        def final_item(m):
+            for jj in range(3):
+                final_bank(m, jj)
+
+        for g in range(3):
+            square_bank(0, g)
+            square_bank(1, g)
+        chain_a(0)
+        regroup_x(0, 1)
+        for g in range(3):
+            square_bank(2, g)
+            square_bank(3, g)
+            if g == 0:
+                chain_b(0)
+                quantise_x(0, 1)
+                regroup_x(1, 0)
+        chain_a(1)
+        for r in range(4, n_tiles + LEAD):
+            if r in (4, 5, 6, 7):
+                final_item(2 * (r - 4))
             for g in range(3):
                 if r < n_tiles:
                     square_bank(r, g)
-                if r >= LEAD:
-                    final_bank(r - LEAD, g)
-            if r == 0:
-                quantise_x(0, 1)
-                regroup_x(1, 0)
-            if r < n_tiles and r % 4 == 3:
-                chain_a()
-            if 0 < r <= n_tiles and r % 4 == 0:
-                chain_b(r // 4 - 1)
-            if r % 4 == 1 and r // 4 + 2 < 2 * B:
-                u = r // 4 + 2
-                quantise_x(u // 2, u % 2)
-                if u + 1 < 2 * B:
-                    regroup_x((u + 1) // 2, (u + 1) % 2)
+                if r >= 4 + LEAD:
+                    final_bank(r - LEAD + 4, g)
+            if r in (4, 5, 6, 7):
+                final_item(2 * (r - 4) + 1)
+            if r == 4:
+                chain_b(1)
+            if 4 < r < n_tiles and r % 4 == 3:
+                chain_a(r // 4 + 1)
+            if 4 < r <= n_tiles and r % 4 == 0:
+                chain_b(r // 4)
+            if r % 4 == 1 and r // 4 < 2 * B - 1:
+                hh = r // 4 + 1
+                quantise_x(hh // 2, hh % 2)
+                if hh + 1 < 2 * B:
+                    regroup_x((hh + 1) // 2, (hh + 1) % 2)

@@ -22,8 +22,8 @@ EPS = 1e-4
 FLOPS = 2 * B * O * C * N
 
 LEAD = 6
-V_TILES = (1, 3, 9, 13, 21)
-G_LAST = 13
+V_TILES = (1, 3)
+G_LAST = 20
 PIN = False
 
 

@@ -22,8 +22,8 @@ EPS = 1e-4
 FLOPS = 2 * B * O * C * N
 
 LEAD = 6
-V_TILES = (1, 3)
-G_LAST = 20
+V_TILES = (1, 3, 5, 13, 21, 27)
+G_FROM = 19
 PIN = False
 
 
@@ -41,12 +41,12 @@ def tile_admattentionblock_pa_t_kernel(tc, x, v_qkv, g_qkv, out):
         nc.scalar.dma_start(out=g_sb[:], in_=g_qkv.rearrange("(p j) -> p j", j=J))
         v_sb = keep.tile([P, J, C], BF16)
         v_view = v_qkv.rearrange("(p j) c -> p j c", j=J)
-        for a in range(3):
-            nc.sync.dma_start(out=v_sb[:, 4 * a:4 * a + 4, :], in_=v_view[:, 4 * a:4 * a + 4, :])
+        for j0, j1 in ((0, 2), (2, 4), (4, 8), (8, 12)):
+            nc.sync.dma_start(out=v_sb[:, j0:j1, :], in_=v_view[:, j0:j1, :])
         x_raw = []
         for b in range(B):
             xr = keep.tile([P, PACK, N], BF16, name="x_raw%d" % b)
-            nc.sync.dma_start(out=xr[:], in_=x[b].rearrange("(p t) h w -> p t (h w)", t=PACK))
+            nc.sync.dma_start(out=xr[:], in_=x[b].rearrange("(t p) h w -> p t (h w)", t=PACK))
             x_raw.append(xr)
 
         ident_bf = keep.tile([P, P], BF16)
@@ -107,20 +107,12 @@ def tile_admattentionblock_pa_t_kernel(tc, x, v_qkv, g_qkv, out):
             nc.vector.tensor_tensor(out=sc[:, four], in0=rnorm[:, four], in1=g_sb[:, four], op=ALU.mult)
             for r in range(4):
                 j = 4 * a + r
-                v_perm = v_sb[:, j, :].rearrange("p (c t) -> p t c", t=PACK)
-                if r < 3:
-                    nc.vector.tensor_scalar(out=w_bf[:, j], in0=v_perm, scalar1=sc[:, j:j + 1],
-                                            scalar2=None, op0=ALU.mult)
-                else:
-                    nc.scalar.activation(out=w_bf[:, j], in_=v_perm, func=ACT.Copy,
-                                         scale=sc[:, j:j + 1])
+                nc.vector.tensor_scalar(out=w_bf[:, j].rearrange("p t c -> p (t c)"), in0=v_sb[:, j, :],
+                                        scalar1=sc[:, j:j + 1], scalar2=None, op0=ALU.mult)
                 wt = psum.tile([P, PACK, P], BF16, tag="mm", bufs=4)
                 for t in range(PACK):
                     nc.tensor.transpose(out=wt[:, t, :], in_=w_bf[:, j, t, :], identity=ident_bf[:])
-                if r == 1:
-                    nc.vector.tensor_copy(out=wg[:, j], in_=wt[:].rearrange("p t o -> p o t"))
-                else:
-                    nc.scalar.copy(out=wg[:, j], in_=wt[:].rearrange("p t o -> p o t"))
+                nc.scalar.copy(out=wg[:, j], in_=wt[:].rearrange("p t o -> p o t"))
             if a == 1:
                 regroup_x(0, 0)
             nc.vector.quantize_mx(
@@ -128,15 +120,11 @@ def tile_admattentionblock_pa_t_kernel(tc, x, v_qkv, g_qkv, out):
                 scales=ws[:, HALF * a:HALF * (a + 1)],
                 in_=wg[:, 4 * a:4 * a + 4].rearrange("p j o t -> p (j o t)"))
         quantise_x(0, 0)
+        regroup_x(0, 1)
+        quantise_x(0, 1)
+        regroup_x(1, 0)
 
         inv_sqrt_o = 1.0 / math.sqrt(O)
-        units = [(0, 0, 2), (0, 2 * P, 2), (0, HALF, 4)]
-        units += [(b, HALF * h, 4) for b in range(1, B) for h in range(2)]
-        unit_of_tile = []
-        for u in range(len(units)):
-            unit_of_tile += [u] * units[u][2]
-        first_tile = [unit_of_tile.index(u) for u in range(len(units))]
-        n_tiles = len(unit_of_tile)
         rb = {}
         accs = {}
         mss = {}
@@ -150,12 +138,10 @@ def tile_admattentionblock_pa_t_kernel(tc, x, v_qkv, g_qkv, out):
 
         def square_bank(k, g):
             b, i = divmod(k, 8)
-            u = unit_of_tile[k]
-            ii = k - first_tile[u]
-            nt = units[u][2]
+            u, ii = divmod(k, 4)
             if u not in accs:
-                accs[u] = work.tile([P, 3 * nt], F32, tag="acc", name="acc")
-                mss[u] = work.tile([P, nt], F32, tag="ms", name="ms")
+                accs[u] = work.tile([P, 12], F32, tag="acc", name="acc")
+                mss[u] = work.tile([P, 4], F32, tag="ms", name="ms")
             on_vector = k in V_TILES
             if on_vector:
                 ps = psum.tile([P, HALF], F32, tag="mm", bufs=4, name="ps_sv")
@@ -179,94 +165,75 @@ def tile_admattentionblock_pa_t_kernel(tc, x, v_qkv, g_qkv, out):
                 first = ii
                 while first > 0 and (k - (ii - first) - 1) not in V_TILES:
                     first -= 1
-                if g == 2 and (ii == nt - 1 or (k + 1) in V_TILES):
+                if g == 2 and (ii == 3 or (k + 1) in V_TILES):
                     nc.vector.tensor_reduce(
                         out=mss[u][:, first:ii + 1],
                         in_=accs[u][:, 3 * first:3 * ii + 3].rearrange("p (i g) -> p i g", g=3),
                         axis=AX.X, op=ALU.add)
 
         def chain_a(u):
-            nt = units[u][2]
-            rms = work.tile([P, nt], F32, tag="rms")
+            rms = work.tile([P, 4], F32, tag="rms")
             nc.scalar.activation(out=rms[:], in_=mss[u][:], func=ACT.Sqrt)
-            rme = work.tile([P, nt], F32, tag="rme")
+            rme = work.tile([P, 4], F32, tag="rme")
             nc.vector.tensor_scalar_add(out=rme[:], in0=rms[:], scalar1=EPS)
-            rinvs[u] = work.tile([P, nt], F32, tag="rinv", name="rinv")
+            rinvs[u] = work.tile([P, 4], F32, tag="rinv", name="rinv")
             nc.vector.reciprocal(out=rinvs[u][:], in_=rme[:])
 
         def chain_b(u):
-            nt = units[u][2]
-            bc = psum.tile([P, P * nt], F32, tag="bc", bufs=1)
-            for q in range(nt):
+            bc = psum.tile([P, HALF], F32, tag="bc", bufs=1)
+            for q in range(4):
                 nc.tensor.transpose(out=bc[:, P * q:P * (q + 1)],
                                     in_=rinvs[u][:, q:q + 1].to_broadcast([P, P]),
                                     identity=ident_f[:])
-            rb[u] = work.tile([P, P * nt], F32, tag="rb", bufs=4, name="rb")
-            if u < 2:
-                nc.vector.tensor_copy(out=rb[u][:], in_=bc[:])
-            else:
-                nc.scalar.copy(out=rb[u][:], in_=bc[:])
+            rb[u] = work.tile([P, HALF], F32, tag="rb", bufs=4, name="rb")
+            nc.scalar.copy(out=rb[u][:], in_=bc[:])
 
-        items = [(u, q) for u in range(len(units)) for q in range(4)]
+        items = [(b, q, h) for b in range(B) for h in range(2) for q in range(4)]
         ots = {}
 
         def final_bank(m, jj):
-            u, q = items[m]
-            b, n0, nt = units[u]
-            width = P * nt
+            b, q, h = items[m]
             j = 3 * q + jj
-            cols = slice(n0, n0 + width)
+            cols = slice(HALF * h, HALF * (h + 1))
             o_view = out[b].rearrange("(p j) n -> p j n", j=J)
             if jj == 0:
-                ots[m] = stage.tile([P, 3, width], F32, tag="ot", name="ot")
+                ots[m] = stage.tile([P, 3, HALF], F32, tag="ot", name="ot")
             dst = ots[m][:, jj, :]
-            ps = psum.tile([P, width], F32, tag="mm", bufs=4, name="ps_mm")
+            ps = psum.tile([P, HALF], F32, tag="mm", bufs=4, name="ps_mm")
             mx(ps, (wc, ws), slice(P * j, P * (j + 1)), (xc[b], xs[b]), cols)
-            if m >= len(items) - G_LAST and jj == 0:
+            if m >= G_FROM and jj == 0:
                 nc.scalar.copy(out=dst, in_=ps[:])
-                nc.gpsimd.tensor_tensor(out=dst, in0=dst, in1=rb[u][:], op=ALU.mult)
+                nc.gpsimd.tensor_tensor(out=dst, in0=dst, in1=rb[2 * b + h][:], op=ALU.mult)
             else:
-                nc.vector.tensor_tensor(out=dst, in0=ps[:], in1=rb[u][:], op=ALU.mult)
+                nc.vector.tensor_tensor(out=dst, in0=ps[:], in1=rb[2 * b + h][:], op=ALU.mult)
             if m == len(items) - 1:
                 nc.sync.dma_start(out=o_view[:, j:j + 1, cols], in_=ots[m][:, jj:jj + 1, :])
             elif jj == 2:
                 nc.sync.dma_start(out=o_view[:, 3 * q:3 * q + 3, cols], in_=ots[m][:])
 
-        def final_item(m):
-            for jj in range(3):
-                final_bank(m, jj)
-
-        for g in range(3):
-            square_bank(0, g)
-            square_bank(1, g)
-        chain_a(0)
-        regroup_x(0, 1)
-        for g in range(3):
-            square_bank(2, g)
-            square_bank(3, g)
-            if g == 0:
-                chain_b(0)
-                quantise_x(0, 1)
-                regroup_x(1, 0)
-        chain_a(1)
-        for r in range(4, n_tiles + LEAD):
-            if r in (4, 5, 6, 7):
-                final_item(2 * (r - 4))
+        n_tiles = 8 * B
+        for k in range(0, LEAD, 2):
+            for g in range(3):
+                square_bank(k, g)
+                square_bank(k + 1, g)
+                if k == 4 and g == 0:
+                    chain_b(0)
+            if k == 2:
+                chain_a(0)
+            if k == 4:
+                quantise_x(1, 0)
+                regroup_x(1, 1)
+        for r in range(LEAD, n_tiles + LEAD):
             for g in range(3):
                 if r < n_tiles:
                     square_bank(r, g)
-                if r >= 4 + LEAD:
-                    final_bank(r - LEAD + 4, g)
-            if r in (4, 5, 6, 7):
-                final_item(2 * (r - 4) + 1)
-            if r == 4:
-                chain_b(1)
-            if 4 < r < n_tiles and r % 4 == 3:
-                chain_a(r // 4 + 1)
-            if 4 < r <= n_tiles and r % 4 == 0:
-                chain_b(r // 4)
+                final_bank(r - LEAD, g)
+            if r < n_tiles and r % 4 == 3:
+                chain_a(r // 4)
+            if r <= n_tiles and r % 4 == 0:
+                chain_b(r // 4 - 1)
             if r % 4 == 1 and r // 4 < 2 * B - 1:
-                hh = r // 4 + 1
-                quantise_x(hh // 2, hh % 2)
-                if hh + 1 < 2 * B:
-                    regroup_x((hh + 1) // 2, (hh + 1) % 2)
+                u = r // 4 + 1
+                quantise_x(u // 2, u % 2)
+                if u + 1 < 2 * B:
+                    regroup_x((u + 1) // 2, (u + 1) % 2)

from contextlib import ExitStack
import math

import concourse.mybir as mybir
from concourse.masks import make_identity

F32 = mybir.dt.float32
BF16 = mybir.dt.bfloat16
U32 = mybir.dt.uint32
U8 = mybir.dt.uint8
FP8X4 = mybir.dt.float8_e4m3fn_x4
ACT = mybir.ActivationFunctionType
ALU = mybir.AluOpType
AX = mybir.AxisListType

B, C, N, O = 4, 512, 1024, 1536
P = 128
PACK = 4
J = O // P
HALF = 512
EPS = 1e-4
FLOPS = 2 * B * O * C * N

LEAD = 6
V_TILES = (1, 3, 5, 13, 21, 27)
G_FROM = 19
PIN = False


def tile_admattentionblock_pa_t_kernel(tc, x, v_qkv, g_qkv, out):
    nc = tc.nc
    with ExitStack() as ctx:
        if PIN:
            ctx.enter_context(tc.manual_schedule())
        keep = ctx.enter_context(tc.tile_pool(name="keep", bufs=1))
        work = ctx.enter_context(tc.tile_pool(name="work", bufs=2))
        stage = ctx.enter_context(tc.tile_pool(name="stage", bufs=8))
        psum = ctx.enter_context(tc.psum_pool(name="psum", bufs=1))

        g_sb = keep.tile([P, J], BF16)
        nc.scalar.dma_start(out=g_sb[:], in_=g_qkv.rearrange("(p j) -> p j", j=J))
        v_sb = keep.tile([P, J, C], BF16)
        v_view = v_qkv.rearrange("(p j) c -> p j c", j=J)
        for j0, j1 in ((0, 2), (2, 4), (4, 8), (8, 12)):
            nc.sync.dma_start(out=v_sb[:, j0:j1, :], in_=v_view[:, j0:j1, :])
        x_raw = []
        for b in range(B):
            xr = keep.tile([P, PACK, N], BF16, name="x_raw%d" % b)
            nc.sync.dma_start(out=xr[:], in_=x[b].rearrange("(t p) h w -> p t (h w)", t=PACK))
            x_raw.append(xr)

        ident_bf = keep.tile([P, P], BF16)
        make_identity(nc, ident_bf[:])
        ident_f = keep.tile([P, P], F32)
        make_identity(nc, ident_f[:])
        one = keep.tile([P, 1], F32)
        nc.vector.memset(one[:], 1.0)
        warm = keep.tile([P, 1], F32)
        nc.scalar.activation(out=warm[:], in_=one[:], func=ACT.Sqrt)

        xc = [keep.tile([P, N], U32, align_bytes=64, name="xc%d" % b) for b in range(B)]
        xs = [keep.tile([P, N], U8, align_bytes=64, name="xs%d" % b) for b in range(B)]
        xgs = {}

        def regroup_x(b, h):
            xg = work.tile([P, HALF, PACK], BF16, align_bytes=64, tag="xg", bufs=1, name="xg")
            src = x_raw[b][:, :, HALF * h:HALF * (h + 1)]
            if b == 0:
                nc.vector.tensor_copy(out=xg[:].rearrange("p (c i) t -> p c t i", i=4),
                                      in_=src.rearrange("p t (c i) -> p c t i", i=4))
            else:
                nc.gpsimd.tensor_scalar(out=xg[:], in0=src.rearrange("p t n -> p n t"),
                                        scalar1=1.0, scalar2=0.0, op0=ALU.mult, op1=ALU.add)
            xgs[(b, h)] = xg

        def quantise_x(b, h):
            nc.vector.quantize_mx(
                out=xc[b][:, HALF * h:HALF * (h + 1)].bitcast(FP8X4),
                scales=xs[b][:, HALF * h:HALF * (h + 1)],
                in_=xgs[(b, h)][:].rearrange("p n t -> p (n t)"))

        ss = keep.tile([P, 3, 16], F32)
        norm = keep.tile([P, J], F32)
        rnorm = keep.tile([P, J], F32)
        sc = keep.tile([P, J], F32)
        w_bf = keep.tile([P, J, PACK, P], BF16)
        wg = keep.tile([P, J, P, PACK], BF16, align_bytes=64)
        wc = keep.tile([P, O], U32, align_bytes=64)
        ws = keep.tile([P, O], U8, align_bytes=64)
        for a in range(3):
            for r in range(4):
                j = 4 * a + r
                if r < 2:
                    junk_s = work.tile([P, C], BF16, tag="junk_s")
                    nc.scalar.activation(out=junk_s[:], in_=v_sb[:, j, :], func=ACT.Square,
                                         accum_out=ss[:, a, r:r + 1])
                else:
                    junk_v = work.tile([P, C], F32, tag="junk_v")
                    nc.vector.scalar_tensor_tensor(out=junk_v[:], in0=v_sb[:, j, :], scalar=1.0,
                                                   in1=v_sb[:, j, :], op0=ALU.mult, op1=ALU.mult,
                                                   accum_out=ss[:, a, 6 + r:7 + r])
            four = slice(4 * a, 4 * a + 4)
            nc.scalar.activation(out=norm[:, four].rearrange("p (s e) -> p s e", e=2),
                                 in_=ss[:, a, :].rearrange("p (s e) -> p s e", e=8)[:, :, 0:2],
                                 func=ACT.Sqrt)
            nc.vector.reciprocal(out=rnorm[:, four], in_=norm[:, four])
            nc.vector.tensor_tensor(out=sc[:, four], in0=rnorm[:, four], in1=g_sb[:, four], op=ALU.mult)
            for r in range(4):
                j = 4 * a + r
                nc.vector.tensor_scalar(out=w_bf[:, j].rearrange("p t c -> p (t c)"), in0=v_sb[:, j, :],
                                        scalar1=sc[:, j:j + 1], scalar2=None, op0=ALU.mult)
                wt = psum.tile([P, PACK, P], BF16, tag="mm", bufs=4)
                for t in range(PACK):
                    nc.tensor.transpose(out=wt[:, t, :], in_=w_bf[:, j, t, :], identity=ident_bf[:])
                nc.scalar.copy(out=wg[:, j], in_=wt[:].rearrange("p t o -> p o t"))
            if a == 1:
                regroup_x(0, 0)
            nc.vector.quantize_mx(
                out=wc[:, HALF * a:HALF * (a + 1)].bitcast(FP8X4),
                scales=ws[:, HALF * a:HALF * (a + 1)],
                in_=wg[:, 4 * a:4 * a + 4].rearrange("p j o t -> p (j o t)"))
        quantise_x(0, 0)
        regroup_x(0, 1)
        quantise_x(0, 1)
        regroup_x(1, 0)

        inv_sqrt_o = 1.0 / math.sqrt(O)
        rb = {}
        accs = {}
        mss = {}
        sts = {}
        rinvs = {}

        def mx(ps, lw, lcols, rw, rcols):
            nc.tensor.matmul_mx(out=ps[:], lhsT=lw[0][:, lcols].bitcast(FP8X4), lhsT_scale=lw[1][:, lcols],
                                rhs=rw[0][:, rcols].bitcast(FP8X4), rhs_scale=rw[1][:, rcols],
                                start=True, stop=True)

        def square_bank(k, g):
            b, i = divmod(k, 8)
            u, ii = divmod(k, 4)
            if u not in accs:
                accs[u] = work.tile([P, 12], F32, tag="acc", name="acc")
                mss[u] = work.tile([P, 4], F32, tag="ms", name="ms")
            on_vector = k in V_TILES
            if on_vector:
                ps = psum.tile([P, HALF], F32, tag="mm", bufs=4, name="ps_sv")
            else:
                ps = psum.tile([P, HALF], F32, tag="sq", bufs=3, name="ps_sq")
            mx(ps, (xc[b], xs[b]), slice(P * i, P * (i + 1)), (wc, ws), slice(HALF * g, HALF * (g + 1)))
            if on_vector:
                if g == 0:
                    sts[k] = work.tile([P, 3, 6], F32, tag="st", name="st")
                nc.vector.bn_stats(out=sts[k][:, g, :], in_=ps[:])
                if g == 2:
                    mv = work.tile([P, 2], F32, tag="mv")
                    nc.vector.bn_aggr(out=mv[:], in_=sts[k][:].rearrange("p g s -> p (g s)"))
                    nc.vector.scalar_tensor_tensor(out=mss[u][:, ii:ii + 1], in0=mv[:, 0:1],
                                                   scalar=mv[:, 0:1], in1=mv[:, 1:2],
                                                   op0=ALU.mult, op1=ALU.add)
            else:
                junk = work.tile([P, HALF], BF16, tag="junk")
                nc.scalar.activation(out=junk[:], in_=ps[:], func=ACT.Square, scale=inv_sqrt_o,
                                     accum_out=accs[u][:, 3 * ii + g:3 * ii + g + 1])
                first = ii
                while first > 0 and (k - (ii - first) - 1) not in V_TILES:
                    first -= 1
                if g == 2 and (ii == 3 or (k + 1) in V_TILES):
                    nc.vector.tensor_reduce(
                        out=mss[u][:, first:ii + 1],
                        in_=accs[u][:, 3 * first:3 * ii + 3].rearrange("p (i g) -> p i g", g=3),
                        axis=AX.X, op=ALU.add)

        def chain_a(u):
            rms = work.tile([P, 4], F32, tag="rms")
            nc.scalar.activation(out=rms[:], in_=mss[u][:], func=ACT.Sqrt)
            rme = work.tile([P, 4], F32, tag="rme")
            nc.vector.tensor_scalar_add(out=rme[:], in0=rms[:], scalar1=EPS)
            rinvs[u] = work.tile([P, 4], F32, tag="rinv", name="rinv")
            nc.vector.reciprocal(out=rinvs[u][:], in_=rme[:])

        def chain_b(u):
            bc = psum.tile([P, HALF], F32, tag="bc", bufs=1)
            for q in range(4):
                nc.tensor.transpose(out=bc[:, P * q:P * (q + 1)],
                                    in_=rinvs[u][:, q:q + 1].to_broadcast([P, P]),
                                    identity=ident_f[:])
            rb[u] = work.tile([P, HALF], F32, tag="rb", bufs=4, name="rb")
            nc.scalar.copy(out=rb[u][:], in_=bc[:])

        items = [(b, q, h) for b in range(B) for h in range(2) for q in range(4)]
        ots = {}

        def final_bank(m, jj):
            b, q, h = items[m]
            j = 3 * q + jj
            cols = slice(HALF * h, HALF * (h + 1))
            o_view = out[b].rearrange("(p j) n -> p j n", j=J)
            if jj == 0:
                ots[m] = stage.tile([P, 3, HALF], F32, tag="ot", name="ot")
            dst = ots[m][:, jj, :]
            ps = psum.tile([P, HALF], F32, tag="mm", bufs=4, name="ps_mm")
            mx(ps, (wc, ws), slice(P * j, P * (j + 1)), (xc[b], xs[b]), cols)
            if m >= G_FROM and jj == 0:
                nc.scalar.copy(out=dst, in_=ps[:])
                nc.gpsimd.tensor_tensor(out=dst, in0=dst, in1=rb[2 * b + h][:], op=ALU.mult)
            else:
                nc.vector.tensor_tensor(out=dst, in0=ps[:], in1=rb[2 * b + h][:], op=ALU.mult)
            if m == len(items) - 1:
                nc.sync.dma_start(out=o_view[:, j:j + 1, cols], in_=ots[m][:, jj:jj + 1, :])
            elif jj == 2:
                nc.sync.dma_start(out=o_view[:, 3 * q:3 * q + 3, cols], in_=ots[m][:])

        n_tiles = 8 * B
        for k in range(0, LEAD, 2):
            for g in range(3):
                square_bank(k, g)
                square_bank(k + 1, g)
                if k == 4 and g == 0:
                    chain_b(0)
            if k == 2:
                chain_a(0)
            if k == 4:
                quantise_x(1, 0)
                regroup_x(1, 1)
        for r in range(LEAD, n_tiles + LEAD):
            for g in range(3):
                if r < n_tiles:
                    square_bank(r, g)
                final_bank(r - LEAD, g)
            if r < n_tiles and r % 4 == 3:
                chain_a(r // 4)
            if r <= n_tiles and r % 4 == 0:
                chain_b(r // 4 - 1)
            if r % 4 == 1 and r // 4 < 2 * B - 1:
                u = r // 4 + 1
                quantise_x(u // 2, u % 2)
                if u + 1 < 2 * B:
                    regroup_x((u + 1) // 2, (u + 1) % 2)
